import numpy as np
import ml_dtypes


def mxq(x, axis, fmt="e4m3"):
    dtype, down = {"e4m3": (ml_dtypes.float8_e4m3fn, 7), "e5m2": (ml_dtypes.float8_e5m2, 14)}[fmt]
    v = np.moveaxis(np.asarray(x, np.float32).astype(ml_dtypes.bfloat16).astype(np.float64), axis, -1)
    blocks = v.reshape(v.shape[:-1] + (-1, 32))
    amax = np.abs(blocks).max(-1, keepdims=True)
    byte = np.maximum(np.where(amax > 0, np.frexp(amax)[1] - 1 + 127, 0) - down, 1)
    scale = np.exp2(byte - 127.0)
    codes = (blocks / scale).astype(np.float32).astype(dtype).astype(np.float64)
    return np.moveaxis((codes * scale).reshape(v.shape), -1, axis)


WIDE = False


def mx_kscale(k):
    if not WIDE:
        return np.ones(k)
    levels = np.array([10, -10, 5, -5, 0])
    a = np.random.permutation(np.resize(levels, k // 512 * 4)).reshape(k // 512, 4)
    idx = np.arange(k)
    return np.exp2(a[idx // 512, idx % 128 // 32])


BF16 = ml_dtypes.bfloat16


def bf(x):
    return np.asarray(x, np.float32).astype(BF16)


def f64(x):
    return np.asarray(x).astype(np.float64)


E2M1 = np.array([0.0, 0.5, 1.0, 1.5, 2.0, 3.0, 4.0, 6.0, -0.0, -0.5, -1.0, -1.5, -2.0, -3.0, -4.0, -6.0])


def pack_weight(w, fmt):
    k, n = w.shape
    w = f64(bf(w)).reshape(k // 32, 32, n)
    amax = np.abs(w).max(1)
    if fmt == "e4m3":
        byte = np.frexp(amax)[1] - 1 + 127 - 7
    else:
        mant, ex = np.frexp(amax / 6.0)
        byte = np.where(mant > 0.5, ex, ex - 1) + 127
    byte = np.clip(np.where(amax > 0, byte, 1), 1, 254)
    scaled = (w * np.exp2(127.0 - byte)[:, None, :]).reshape(k, n).astype(np.float32)
    by_word = np.ascontiguousarray(scaled.reshape(k // 512, 128, 4, n).transpose(0, 1, 3, 2))
    if fmt == "e4m3":
        words = by_word.astype(ml_dtypes.float8_e4m3fn).view(np.uint8)
    else:
        c = by_word.astype(ml_dtypes.float4_e2m1fn).view(np.uint8) & 0xF
        words = c[..., 0::2] | (c[..., 1::2] << 4)
    return np.ascontiguousarray(words), np.ascontiguousarray(byte.astype(np.uint8).reshape(k // 512, 16, n))


def unpack_weight(words, scales, fmt):
    g, p, n, _ = words.shape
    if fmt == "e4m3":
        vals = np.ascontiguousarray(words).view(ml_dtypes.float8_e4m3fn).astype(np.float64)
    else:
        nib = np.empty((g, p, n, 4), np.uint8)
        nib[..., 0::2] = words & 0xF
        nib[..., 1::2] = words >> 4
        vals = E2M1[nib]
    vals = vals * np.repeat(np.exp2(scales.astype(np.float64) - 127.0), 8, axis=1)[..., None]
    return vals.transpose(0, 1, 3, 2).reshape(g * 512, n)

def pack4(w):
    words, scales = pack_weight(w, "e2m1")
    return words.reshape(words.shape[0], 128, -1), scales


def unpack4(words, scales):
    return unpack_weight(words.reshape(words.shape[0], 128, -1, 2), scales, "e2m1")


B, D = 128, 1024


def softplus(v):
    return np.logaddexp(v, 0.0)


def setup_inputs():
    s = mx_kscale(D)
    xt = bf(np.random.standard_normal((B, D)) * 1.3 * s)
    eps = bf(np.random.standard_normal((B, D)))
    x = bf(np.random.standard_normal((B, D)))
    t_rand = bf(np.random.uniform(0.0, 1.0, (B, 1)))
    Wm_words, Wm_scales = pack4((np.random.standard_normal((D, D)) / np.sqrt(D) / s[None, :]).T)
    bm = bf(np.random.standard_normal(D) * 0.5)
    Wv_words, Wv_scales = pack4((np.random.standard_normal((D, D)) / np.sqrt(D) / s[None, :]).T)
    bv = bf(np.random.standard_normal(D) * 0.5)
    return {"xt": xt, "eps": eps, "x": x, "t_rand": t_rand,
            "Wm_words": Wm_words, "Wm_scales": Wm_scales, "bm": bm,
            "Wv_words": Wv_words, "Wv_scales": Wv_scales, "bv": bv}


def reference(xt, eps, x, t_rand, Wm_words, Wm_scales, bm, Wv_words, Wv_scales, bv):
    xq = mxq(f64(xt), 1, "e4m3")
    mu = (xq @ unpack4(Wm_words, Wm_scales)) + f64(bm)
    sigma = softplus((xq @ unpack4(Wv_words, Wv_scales)) + f64(bv))
    x_prime = mu + sigma * f64(eps)
    return (1.0 - f64(t_rand)) * f64(x) + f64(t_rand) * x_prime

@@ -1,0 +1,160 @@
+from contextlib import ExitStack
+
+import concourse.mybir as mybir
+from concourse.masks import make_identity
+
+F32 = mybir.dt.float32
+BF16 = mybir.dt.bfloat16
+I32 = mybir.dt.int32
+U32 = mybir.dt.uint32
+U8 = mybir.dt.uint8
+FP8X4 = mybir.dt.float8_e4m3fn_x4
+FP4X4 = mybir.dt.float4_e2m1fn_x4
+ALU = mybir.AluOpType
+ACT = mybir.ActivationFunctionType
+
+P = 128
+D = 1024
+PACK = 4
+K_PASS = P * PACK
+PASSES = D // K_PASS
+N_TILE = 512
+N_TILES = D // N_TILE
+WORDS_PASS = K_PASS // 2
+SCALE_ROWS = 4
+
+FLOPS = 2 * 2 * P * D * D
+
+
+def load_weight(nc, keep, words_dram, scales_dram, label):
+    planes = keep.tile([P, PASSES, D], U8, name=label + "_planes", align_bytes=64)
+    words = keep.tile([P, PASSES, 2 * D], U8, name=label + "_words", align_bytes=64)
+    nc.vector.memset(planes[:].bitcast(I32), 0)
+    rows = scales_dram.bitcast(I32).rearrange("g (q r) n -> r q g n", r=SCALE_ROWS)
+    for r in range(SCALE_ROWS):
+        nc.sync.dma_start(out=planes[r:P:32].bitcast(I32), in_=rows[r])
+    nc.sync.dma_start(
+        out=words[:].bitcast(I32), in_=words_dram.bitcast(I32).rearrange("g p w -> p g w")
+    )
+    return words, planes
+
+
+def product(nc, psum, xq_codes, xq_scales, words, planes, label):
+    banks = []
+    for h in range(N_TILES):
+        bank = psum.tile([P, N_TILE], F32, name="%s_bank%d" % (label, h))
+        for g in range(PASSES):
+            nc.tensor.matmul_mx(
+                out=bank[:],
+                lhsT=xq_codes[:, g, :].bitcast(FP8X4),
+                lhsT_scale=xq_scales[:, g, :],
+                rhs=words[:, g, 2 * N_TILE * h : 2 * N_TILE * (h + 1)].bitcast(FP4X4),
+                rhs_scale=planes[:, g, N_TILE * h : N_TILE * (h + 1)],
+                start=(g == 0),
+                stop=(g == PASSES - 1),
+            )
+        banks.append(bank)
+    return banks
+
+
+def tile_diffscm_pb_s_kernel(
+    tc, xt, eps, x, t_rand, Wm_words, Wm_scales, bm, Wv_words, Wv_scales, bv, out
+):
+    nc = tc.nc
+    with ExitStack() as ctx:
+        keep = ctx.enter_context(tc.tile_pool(name="keep", bufs=1))
+        psum = ctx.enter_context(tc.psum_pool(name="psum", bufs=1))
+
+        xt_sb = keep.tile([P, D], BF16)
+        nc.scalar.dma_start(out=xt_sb[:], in_=xt)
+        wv_words, wv_planes = load_weight(nc, keep, Wv_words, Wv_scales, "wv")
+        t_bf = keep.tile([P, 1], BF16)
+        nc.scalar.dma_start(out=t_bf[:], in_=t_rand)
+        bv_all = keep.tile([P, D], BF16)
+        nc.scalar.dma_start(out=bv_all[:], in_=bv.partition_broadcast(P))
+        eps_sb = keep.tile([P, D], BF16)
+        nc.scalar.dma_start(out=eps_sb[:], in_=eps)
+        x_sb = keep.tile([P, D], BF16)
+        nc.scalar.dma_start(out=x_sb[:], in_=x)
+        bm_all = keep.tile([P, D], BF16)
+        nc.scalar.dma_start(out=bm_all[:], in_=bm.partition_broadcast(P))
+        wm_words, wm_planes = load_weight(nc, keep, Wm_words, Wm_scales, "wm")
+
+        ident = keep.tile([P, P], F32)
+        make_identity(nc, ident[:])
+        xt_words = xt_sb[:].bitcast(F32)
+        xt_ps = psum.tile([P, PASSES, 2, P], F32)
+        for g in range(PASSES):
+            for u in range(2):
+                nc.tensor.transpose(
+                    xt_ps[:, g, u, :],
+                    xt_words[:, WORDS_PASS * g + u : WORDS_PASS * (g + 1) : 2],
+                    ident[:],
+                )
+        grouped = keep.tile([P, PASSES, P, PACK], BF16, align_bytes=64)
+        nc.vector.tensor_copy(
+            out=grouped[:].bitcast(F32), in_=xt_ps[:].rearrange("p g u b -> p g b u")
+        )
+        xq_codes = keep.tile([P, PASSES, P], U32, align_bytes=64)
+        xq_scales = keep.tile([P, PASSES, P], U8, align_bytes=64)
+        nc.vector.quantize_mx(
+            out=xq_codes[:].rearrange("p g b -> p (g b)").bitcast(FP8X4),
+            scales=xq_scales[:].rearrange("p g b -> p (g b)"),
+            in_=grouped[:].rearrange("p g b t -> p (g b t)"),
+        )
+
+        v_banks = product(nc, psum, xq_codes, xq_scales, wv_words, wv_planes, "v")
+        m_banks = product(nc, psum, xq_codes, xq_scales, wm_words, wm_planes, "m")
+
+        t32 = keep.tile([P, 1], F32)
+        nc.vector.tensor_copy(out=t32[:], in_=t_bf[:])
+        one_minus_t = keep.tile([P, 1], F32)
+        nc.vector.tensor_scalar(
+            out=one_minus_t[:], in0=t_bf[:], scalar1=-1.0, scalar2=1.0, op0=ALU.mult, op1=ALU.add
+        )
+        t_eps = keep.tile([P, D], F32)
+        nc.scalar.activation(out=t_eps[:], in_=eps_sb[:], func=ACT.Copy, scale=t32[:, 0:1])
+        t_bm = keep.tile([P, D], F32)
+        nc.scalar.activation(out=t_bm[:], in_=bm_all[:], func=ACT.Copy, scale=t32[:, 0:1])
+        base = keep.tile([P, D], F32)
+        nc.vector.scalar_tensor_tensor(
+            out=base[:], in0=x_sb[:], scalar=one_minus_t[:, 0:1], in1=t_bm[:],
+            op0=ALU.mult, op1=ALU.add,
+        )
+
+        halves = [slice(N_TILE * h, N_TILE * (h + 1)) for h in range(N_TILES)]
+        v = keep.tile([P, D], F32)
+        abs_v = keep.tile([P, D], F32)
+        exp_v = keep.tile([P, D], F32)
+        log_v = keep.tile([P, D], F32)
+        ramp = keep.tile([P, D], F32)
+        mean = keep.tile([P, D], F32)
+        rest = keep.tile([P, D], F32)
+        tail = keep.tile([P, D], F32)
+        result = keep.tile([P, D], F32)
+        for h, cols in enumerate(halves):
+            nc.vector.tensor_tensor(out=v[:, cols], in0=v_banks[h][:], in1=bv_all[:, cols], op=ALU.add)
+        for cols in halves:
+            nc.scalar.activation(out=abs_v[:, cols], in_=v[:, cols], func=ACT.Abs)
+        for cols in halves:
+            nc.scalar.activation(out=exp_v[:, cols], in_=abs_v[:, cols], func=ACT.Exp, scale=-1.0)
+        for cols in halves:
+            nc.scalar.activation(out=log_v[:, cols], in_=exp_v[:, cols], func=ACT.Ln, bias=1.0)
+
+        for cols in halves:
+            nc.vector.scalar_tensor_tensor(
+                out=ramp[:, cols], in0=v[:, cols], scalar=0.0, in1=t_eps[:, cols],
+                op0=ALU.max, op1=ALU.mult,
+            )
+        for h, cols in enumerate(halves):
+            nc.vector.scalar_tensor_tensor(
+                out=mean[:, cols], in0=m_banks[h][:], scalar=t32[:, 0:1], in1=base[:, cols],
+                op0=ALU.mult, op1=ALU.add,
+            )
+        for cols in halves:
+            nc.vector.tensor_tensor(out=rest[:, cols], in0=mean[:, cols], in1=ramp[:, cols], op=ALU.add)
+        for cols in halves:
+            nc.vector.tensor_tensor(out=tail[:, cols], in0=log_v[:, cols], in1=t_eps[:, cols], op=ALU.mult)
+        for cols in halves:
+            nc.vector.tensor_tensor(out=result[:, cols], in0=tail[:, cols], in1=rest[:, cols], op=ALU.add)
+            nc.sync.dma_start(out=out[:, cols], in_=result[:, cols])

@@ -22,6 +22,7 @@ N_TILE = 512
 N_TILES = D // N_TILE
 WORDS_PASS = K_PASS // 2
 SCALE_ROWS = 4
+BIAS_ROWS = D // (2 * P)
 
 FLOPS = 2 * 2 * P * D * D
 
@@ -64,24 +65,43 @@ def tile_diffscm_pb_s_kernel(
     with ExitStack() as ctx:
         keep = ctx.enter_context(tc.tile_pool(name="keep", bufs=1))
         psum = ctx.enter_context(tc.psum_pool(name="psum", bufs=1))
+        ctx.enter_context(tc.manual_schedule())
 
         xt_sb = keep.tile([P, D], BF16)
-        nc.scalar.dma_start(out=xt_sb[:], in_=xt)
+        nc.sync.dma_start(out=xt_sb[:], in_=xt)
+        bias_rows = keep.tile([P, 2 * P], BF16)
+        nc.vector.memset(bias_rows[:].bitcast(I32), 0)
+        nc.sync.dma_start(out=bias_rows[0:BIAS_ROWS, :], in_=bv.rearrange("(r c) -> r c", r=BIAS_ROWS))
+        nc.sync.dma_start(
+            out=bias_rows[BIAS_ROWS : 2 * BIAS_ROWS, :], in_=bm.rearrange("(r c) -> r c", r=BIAS_ROWS)
+        )
         wv_words, wv_planes = load_weight(nc, keep, Wv_words, Wv_scales, "wv")
         t_bf = keep.tile([P, 1], BF16)
-        nc.scalar.dma_start(out=t_bf[:], in_=t_rand)
-        bv_all = keep.tile([P, D], BF16)
-        nc.scalar.dma_start(out=bv_all[:], in_=bv.partition_broadcast(P))
+        nc.sync.dma_start(out=t_bf[:], in_=t_rand)
         eps_sb = keep.tile([P, D], BF16)
-        nc.scalar.dma_start(out=eps_sb[:], in_=eps)
+        nc.sync.dma_start(out=eps_sb[:], in_=eps)
         x_sb = keep.tile([P, D], BF16)
-        nc.scalar.dma_start(out=x_sb[:], in_=x)
-        bm_all = keep.tile([P, D], BF16)
-        nc.scalar.dma_start(out=bm_all[:], in_=bm.partition_broadcast(P))
+        nc.sync.dma_start(out=x_sb[:], in_=x)
         wm_words, wm_planes = load_weight(nc, keep, Wm_words, Wm_scales, "wm")
 
         ident = keep.tile([P, P], F32)
         make_identity(nc, ident[:])
+        t32 = keep.tile([P, 1], F32)
+        nc.gpsimd.tensor_copy(out=t32[:], in_=t_bf[:])
+        one_minus_t = keep.tile([P, 1], F32)
+        nc.gpsimd.tensor_scalar(
+            out=one_minus_t[:], in0=t_bf[:], scalar1=-1.0, scalar2=1.0, op0=ALU.mult, op1=ALU.add
+        )
+        t_eps = keep.tile([P, D], F32)
+        nc.gpsimd.tensor_scalar(
+            out=t_eps[:], in0=eps_sb[:], scalar1=t32[:, 0:1], scalar2=0.0, op0=ALU.mult, op1=ALU.add
+        )
+        x_part = keep.tile([P, D], F32)
+        nc.gpsimd.tensor_scalar(
+            out=x_part[:], in0=x_sb[:], scalar1=one_minus_t[:, 0:1], scalar2=0.0,
+            op0=ALU.mult, op1=ALU.add,
+        )
+
         xt_words = xt_sb[:].bitcast(F32)
         xt_ps = psum.tile([P, PASSES, 2, P], F32)
         for g in range(PASSES):
@@ -91,10 +111,15 @@ def tile_diffscm_pb_s_kernel(
                     xt_words[:, WORDS_PASS * g + u : WORDS_PASS * (g + 1) : 2],
                     ident[:],
                 )
+        bias_cols_ps = psum.tile([P, P], F32)
+        nc.tensor.transpose(bias_cols_ps[:], bias_rows[:].bitcast(F32), ident[:])
+
         grouped = keep.tile([P, PASSES, P, PACK], BF16, align_bytes=64)
         nc.vector.tensor_copy(
             out=grouped[:].bitcast(F32), in_=xt_ps[:].rearrange("p g u b -> p g b u")
         )
+        bias_cols = keep.tile([P, 2 * BIAS_ROWS], F32)
+        nc.vector.tensor_copy(out=bias_cols[:], in_=bias_cols_ps[:, 0 : 2 * BIAS_ROWS])
         xq_codes = keep.tile([P, PASSES, P], U32, align_bytes=64)
         xq_scales = keep.tile([P, PASSES, P], U8, align_bytes=64)
         nc.vector.quantize_mx(
@@ -103,35 +128,25 @@ def tile_diffscm_pb_s_kernel(
             in_=grouped[:].rearrange("p g b t -> p (g b t)"),
         )
 
-        v_banks = product(nc, psum, xq_codes, xq_scales, wv_words, wv_planes, "v")
-        m_banks = product(nc, psum, xq_codes, xq_scales, wm_words, wm_planes, "m")
+        def spread_bias(first_row, label):
+            bank = psum.tile([P, BIAS_ROWS, P], F32, name=label + "_ps")
+            for r in range(BIAS_ROWS):
+                column = bias_cols[:, first_row + r : first_row + r + 1]
+                nc.tensor.transpose(bank[:, r, :], column.to_broadcast([P, P]), ident[:])
+            return bank[:].rearrange("p r j -> p (r j)")
 
-        t32 = keep.tile([P, 1], F32)
-        nc.vector.tensor_copy(out=t32[:], in_=t_bf[:])
-        one_minus_t = keep.tile([P, 1], F32)
-        nc.vector.tensor_scalar(
-            out=one_minus_t[:], in0=t_bf[:], scalar1=-1.0, scalar2=1.0, op0=ALU.mult, op1=ALU.add
-        )
-        t_eps = keep.tile([P, D], F32)
-        nc.scalar.activation(out=t_eps[:], in_=eps_sb[:], func=ACT.Copy, scale=t32[:, 0:1])
-        t_bm = keep.tile([P, D], F32)
-        nc.scalar.activation(out=t_bm[:], in_=bm_all[:], func=ACT.Copy, scale=t32[:, 0:1])
-        base = keep.tile([P, D], F32)
-        nc.vector.scalar_tensor_tensor(
-            out=base[:], in0=x_sb[:], scalar=one_minus_t[:, 0:1], in1=t_bm[:],
-            op0=ALU.mult, op1=ALU.add,
-        )
+        bv_ps = spread_bias(0, "bv")
+        bv_all = keep.tile([P, D], BF16)
+        nc.scalar.copy(out=bv_all[:].bitcast(F32), in_=bv_ps)
+        v_banks = product(nc, psum, xq_codes, xq_scales, wv_words, wv_planes, "v")
+        bm_ps = spread_bias(BIAS_ROWS, "bm")
+        m_banks = product(nc, psum, xq_codes, xq_scales, wm_words, wm_planes, "m")
 
         halves = [slice(N_TILE * h, N_TILE * (h + 1)) for h in range(N_TILES)]
         v = keep.tile([P, D], F32)
         abs_v = keep.tile([P, D], F32)
         exp_v = keep.tile([P, D], F32)
         log_v = keep.tile([P, D], F32)
-        ramp = keep.tile([P, D], F32)
-        mean = keep.tile([P, D], F32)
-        rest = keep.tile([P, D], F32)
-        tail = keep.tile([P, D], F32)
-        result = keep.tile([P, D], F32)
         for h, cols in enumerate(halves):
             nc.vector.tensor_tensor(out=v[:, cols], in0=v_banks[h][:], in1=bv_all[:, cols], op=ALU.add)
         for cols in halves:
@@ -141,10 +156,21 @@ def tile_diffscm_pb_s_kernel(
         for cols in halves:
             nc.scalar.activation(out=log_v[:, cols], in_=exp_v[:, cols], func=ACT.Ln, bias=1.0)
 
+        ramp = keep.tile([P, D], F32)
+        base = keep.tile([P, D], F32)
+        mean = keep.tile([P, D], F32)
+        rest = keep.tile([P, D], F32)
+        tail = keep.tile([P, D], F32)
+        result = keep.tile([P, D], F32)
         for cols in halves:
             nc.vector.scalar_tensor_tensor(
                 out=ramp[:, cols], in0=v[:, cols], scalar=0.0, in1=t_eps[:, cols],
                 op0=ALU.max, op1=ALU.mult,
+            )
+        for cols in halves:
+            nc.vector.scalar_tensor_tensor(
+                out=base[:, cols], in0=bm_ps.bitcast(BF16)[:, cols], scalar=t32[:, 0:1],
+                in1=x_part[:, cols], op0=ALU.mult, op1=ALU.add,
             )
         for h, cols in enumerate(halves):
             nc.vector.scalar_tensor_tensor(

@@ -75,9 +75,9 @@ def tile_diffscm_pb_s_kernel(
         nc.sync.dma_start(
             out=bias_rows[BIAS_ROWS : 2 * BIAS_ROWS, :], in_=bm.rearrange("(r c) -> r c", r=BIAS_ROWS)
         )
-        wv_words, wv_planes = load_weight(nc, keep, Wv_words, Wv_scales, "wv")
         t_bf = keep.tile([P, 1], BF16)
         nc.sync.dma_start(out=t_bf[:], in_=t_rand)
+        wv_words, wv_planes = load_weight(nc, keep, Wv_words, Wv_scales, "wv")
         eps_sb = keep.tile([P, D], BF16)
         nc.sync.dma_start(out=eps_sb[:], in_=eps)
         x_sb = keep.tile([P, D], BF16)
@@ -91,15 +91,6 @@ def tile_diffscm_pb_s_kernel(
         one_minus_t = keep.tile([P, 1], F32)
         nc.gpsimd.tensor_scalar(
             out=one_minus_t[:], in0=t_bf[:], scalar1=-1.0, scalar2=1.0, op0=ALU.mult, op1=ALU.add
-        )
-        t_eps = keep.tile([P, D], F32)
-        nc.gpsimd.tensor_scalar(
-            out=t_eps[:], in0=eps_sb[:], scalar1=t32[:, 0:1], scalar2=0.0, op0=ALU.mult, op1=ALU.add
-        )
-        x_part = keep.tile([P, D], F32)
-        nc.gpsimd.tensor_scalar(
-            out=x_part[:], in0=x_sb[:], scalar1=one_minus_t[:, 0:1], scalar2=0.0,
-            op0=ALU.mult, op1=ALU.add,
         )
 
         xt_words = xt_sb[:].bitcast(F32)
@@ -138,8 +129,10 @@ def tile_diffscm_pb_s_kernel(
         bv_ps = spread_bias(0, "bv")
         bv_all = keep.tile([P, D], BF16)
         nc.scalar.copy(out=bv_all[:].bitcast(F32), in_=bv_ps)
-        v_banks = product(nc, psum, xq_codes, xq_scales, wv_words, wv_planes, "v")
         bm_ps = spread_bias(BIAS_ROWS, "bm")
+        t_bm = keep.tile([P, D], F32)
+        nc.scalar.activation(out=t_bm[:], in_=bm_ps.bitcast(BF16), func=ACT.Copy, scale=t32[:, 0:1])
+        v_banks = product(nc, psum, xq_codes, xq_scales, wv_words, wv_planes, "v")
         m_banks = product(nc, psum, xq_codes, xq_scales, wm_words, wm_planes, "m")
 
         halves = [slice(N_TILE * h, N_TILE * (h + 1)) for h in range(N_TILES)]
@@ -164,13 +157,13 @@ def tile_diffscm_pb_s_kernel(
         result = keep.tile([P, D], F32)
         for cols in halves:
             nc.vector.scalar_tensor_tensor(
-                out=ramp[:, cols], in0=v[:, cols], scalar=0.0, in1=t_eps[:, cols],
+                out=ramp[:, cols], in0=v[:, cols], scalar=0.0, in1=eps_sb[:, cols],
                 op0=ALU.max, op1=ALU.mult,
             )
         for cols in halves:
             nc.vector.scalar_tensor_tensor(
-                out=base[:, cols], in0=bm_ps.bitcast(BF16)[:, cols], scalar=t32[:, 0:1],
-                in1=x_part[:, cols], op0=ALU.mult, op1=ALU.add,
+                out=base[:, cols], in0=x_sb[:, cols], scalar=one_minus_t[:, 0:1],
+                in1=t_bm[:, cols], op0=ALU.mult, op1=ALU.add,
             )
         for h, cols in enumerate(halves):
             nc.vector.scalar_tensor_tensor(
@@ -178,9 +171,15 @@ def tile_diffscm_pb_s_kernel(
                 op0=ALU.mult, op1=ALU.add,
             )
         for cols in halves:
-            nc.vector.tensor_tensor(out=rest[:, cols], in0=mean[:, cols], in1=ramp[:, cols], op=ALU.add)
+            nc.vector.scalar_tensor_tensor(
+                out=rest[:, cols], in0=ramp[:, cols], scalar=t32[:, 0:1], in1=mean[:, cols],
+                op0=ALU.mult, op1=ALU.add,
+            )
         for cols in halves:
-            nc.vector.tensor_tensor(out=tail[:, cols], in0=log_v[:, cols], in1=t_eps[:, cols], op=ALU.mult)
+            nc.vector.scalar_tensor_tensor(
+                out=tail[:, cols], in0=log_v[:, cols], scalar=t32[:, 0:1], in1=eps_sb[:, cols],
+                op0=ALU.mult, op1=ALU.mult,
+            )
         for cols in halves:
             nc.vector.tensor_tensor(out=result[:, cols], in0=tail[:, cols], in1=rest[:, cols], op=ALU.add)
             nc.sync.dma_start(out=out[:, cols], in_=result[:, cols])

@@ -78,14 +78,14 @@ def tile_diffscm_pb_s_kernel(
         t_bf = keep.tile([P, 1], BF16)
         nc.sync.dma_start(out=t_bf[:], in_=t_rand)
         wv_words, wv_planes = load_weight(nc, keep, Wv_words, Wv_scales, "wv")
-        eps_sb = keep.tile([P, D], BF16)
-        nc.sync.dma_start(out=eps_sb[:], in_=eps)
-        x_sb = keep.tile([P, D], BF16)
-        nc.sync.dma_start(out=x_sb[:], in_=x)
         wm_words, wm_planes = load_weight(nc, keep, Wm_words, Wm_scales, "wm")
 
         ident = keep.tile([P, P], F32)
         make_identity(nc, ident[:])
+        eps_sb = keep.tile([P, D], BF16)
+        nc.gpsimd.dma_start(out=eps_sb[:], in_=eps)
+        x_sb = keep.tile([P, D], BF16)
+        nc.gpsimd.dma_start(out=x_sb[:], in_=x)
         t32 = keep.tile([P, 1], F32)
         nc.gpsimd.tensor_copy(out=t32[:], in_=t_bf[:])
         one_minus_t = keep.tile([P, 1], F32)

@@ -87,9 +87,9 @@ def tile_diffscm_pb_s_kernel(
         x_sb = keep.tile([P, D], BF16)
         nc.gpsimd.dma_start(out=x_sb[:], in_=x)
         t32 = keep.tile([P, 1], F32)
-        nc.gpsimd.tensor_copy(out=t32[:], in_=t_bf[:])
+        nc.vector.tensor_copy(out=t32[:], in_=t_bf[:])
         one_minus_t = keep.tile([P, 1], F32)
-        nc.gpsimd.tensor_scalar(
+        nc.vector.tensor_scalar(
             out=one_minus_t[:], in0=t_bf[:], scalar1=-1.0, scalar2=1.0, op0=ALU.mult, op1=ALU.add
         )
 

@@ -75,9 +75,9 @@ def tile_diffscm_pb_s_kernel(
         nc.sync.dma_start(
             out=bias_rows[BIAS_ROWS : 2 * BIAS_ROWS, :], in_=bm.rearrange("(r c) -> r c", r=BIAS_ROWS)
         )
+        wv_words, wv_planes = load_weight(nc, keep, Wv_words, Wv_scales, "wv")
         t_bf = keep.tile([P, 1], BF16)
         nc.sync.dma_start(out=t_bf[:], in_=t_rand)
-        wv_words, wv_planes = load_weight(nc, keep, Wv_words, Wv_scales, "wv")
         wm_words, wm_planes = load_weight(nc, keep, Wm_words, Wm_scales, "wm")
 
         ident = keep.tile([P, P], F32)
@@ -86,13 +86,9 @@ def tile_diffscm_pb_s_kernel(
         nc.gpsimd.dma_start(out=eps_sb[:], in_=eps)
         x_sb = keep.tile([P, D], BF16)
         nc.gpsimd.dma_start(out=x_sb[:], in_=x)
-        t32 = keep.tile([P, 1], F32)
-        nc.vector.tensor_copy(out=t32[:], in_=t_bf[:])
-        one_minus_t = keep.tile([P, 1], F32)
-        nc.vector.tensor_scalar(
-            out=one_minus_t[:], in0=t_bf[:], scalar1=-1.0, scalar2=1.0, op0=ALU.mult, op1=ALU.add
-        )
 
+        bias_cols_ps = psum.tile([P, P], F32)
+        nc.tensor.transpose(bias_cols_ps[:], bias_rows[:].bitcast(F32), ident[:])
         xt_words = xt_sb[:].bitcast(F32)
         xt_ps = psum.tile([P, PASSES, 2, P], F32)
         for g in range(PASSES):
@@ -102,21 +98,26 @@ def tile_diffscm_pb_s_kernel(
                     xt_words[:, WORDS_PASS * g + u : WORDS_PASS * (g + 1) : 2],
                     ident[:],
                 )
-        bias_cols_ps = psum.tile([P, P], F32)
-        nc.tensor.transpose(bias_cols_ps[:], bias_rows[:].bitcast(F32), ident[:])
+        bias_cols = keep.tile([P, 2 * BIAS_ROWS], F32)
+        nc.scalar.copy(out=bias_cols[:], in_=bias_cols_ps[:, 0 : 2 * BIAS_ROWS])
 
         grouped = keep.tile([P, PASSES, P, PACK], BF16, align_bytes=64)
         nc.vector.tensor_copy(
             out=grouped[:].bitcast(F32), in_=xt_ps[:].rearrange("p g u b -> p g b u")
         )
-        bias_cols = keep.tile([P, 2 * BIAS_ROWS], F32)
-        nc.vector.tensor_copy(out=bias_cols[:], in_=bias_cols_ps[:, 0 : 2 * BIAS_ROWS])
         xq_codes = keep.tile([P, PASSES, P], U32, align_bytes=64)
         xq_scales = keep.tile([P, PASSES, P], U8, align_bytes=64)
         nc.vector.quantize_mx(
             out=xq_codes[:].rearrange("p g b -> p (g b)").bitcast(FP8X4),
             scales=xq_scales[:].rearrange("p g b -> p (g b)"),
             in_=grouped[:].rearrange("p g b t -> p (g b t)"),
+        )
+
+        t32 = keep.tile([P, 1], F32)
+        nc.vector.tensor_copy(out=t32[:], in_=t_bf[:])
+        one_minus_t = keep.tile([P, 1], F32)
+        nc.vector.tensor_scalar(
+            out=one_minus_t[:], in0=t_bf[:], scalar1=-1.0, scalar2=1.0, op0=ALU.mult, op1=ALU.add
         )
 
         def spread_bias(first_row, label):

@@ -152,7 +152,7 @@ def tile_diffscm_pb_s_kernel(
 
         ramp = keep.tile([P, D], F32)
         base = keep.tile([P, D], F32)
-        mean = keep.tile([P, D], F32)
+        side = keep.tile([P, D], F32)
         rest = keep.tile([P, D], F32)
         tail = keep.tile([P, D], F32)
         result = keep.tile([P, D], F32)
@@ -166,14 +166,14 @@ def tile_diffscm_pb_s_kernel(
                 out=base[:, cols], in0=x_sb[:, cols], scalar=one_minus_t[:, 0:1],
                 in1=t_bm[:, cols], op0=ALU.mult, op1=ALU.add,
             )
-        for h, cols in enumerate(halves):
-            nc.vector.scalar_tensor_tensor(
-                out=mean[:, cols], in0=m_banks[h][:], scalar=t32[:, 0:1], in1=base[:, cols],
-                op0=ALU.mult, op1=ALU.add,
-            )
         for cols in halves:
             nc.vector.scalar_tensor_tensor(
-                out=rest[:, cols], in0=ramp[:, cols], scalar=t32[:, 0:1], in1=mean[:, cols],
+                out=side[:, cols], in0=ramp[:, cols], scalar=t32[:, 0:1], in1=base[:, cols],
+                op0=ALU.mult, op1=ALU.add,
+            )
+        for h, cols in enumerate(halves):
+            nc.vector.scalar_tensor_tensor(
+                out=rest[:, cols], in0=m_banks[h][:], scalar=t32[:, 0:1], in1=side[:, cols],
                 op0=ALU.mult, op1=ALU.add,
             )
         for cols in halves:

@@ -82,10 +82,18 @@ def tile_diffscm_pb_s_kernel(
 
         ident = keep.tile([P, P], F32)
         make_identity(nc, ident[:])
-        eps_sb = keep.tile([P, D], BF16)
-        nc.gpsimd.dma_start(out=eps_sb[:], in_=eps)
         x_sb = keep.tile([P, D], BF16)
         nc.gpsimd.dma_start(out=x_sb[:], in_=x)
+        eps_sb = keep.tile([P, D], BF16)
+        nc.gpsimd.dma_start(out=eps_sb[:], in_=eps)
+        one_minus_t = keep.tile([P, 1], F32)
+        nc.gpsimd.tensor_scalar(
+            out=one_minus_t[:], in0=t_bf[:], scalar1=-1.0, scalar2=1.0, op0=ALU.mult, op1=ALU.add
+        )
+        x_part = keep.tile([P, D], F32)
+        nc.gpsimd.tensor_scalar(
+            out=x_part[:], in0=x_sb[:], scalar1=one_minus_t[:, 0:1], scalar2=0.0, op0=ALU.mult, op1=ALU.add
+        )
 
         bias_cols_ps = psum.tile([P, P], F32)
         nc.tensor.transpose(bias_cols_ps[:], bias_rows[:].bitcast(F32), ident[:])
@@ -113,13 +121,6 @@ def tile_diffscm_pb_s_kernel(
             in_=grouped[:].rearrange("p g b t -> p (g b t)"),
         )
 
-        t32 = keep.tile([P, 1], F32)
-        nc.vector.tensor_copy(out=t32[:], in_=t_bf[:])
-        one_minus_t = keep.tile([P, 1], F32)
-        nc.vector.tensor_scalar(
-            out=one_minus_t[:], in0=t_bf[:], scalar1=-1.0, scalar2=1.0, op0=ALU.mult, op1=ALU.add
-        )
-
         def spread_bias(first_row, label):
             bank = psum.tile([P, BIAS_ROWS, P], F32, name=label + "_ps")
             for r in range(BIAS_ROWS):
@@ -131,8 +132,6 @@ def tile_diffscm_pb_s_kernel(
         bv_all = keep.tile([P, D], BF16)
         nc.scalar.copy(out=bv_all[:].bitcast(F32), in_=bv_ps)
         bm_ps = spread_bias(BIAS_ROWS, "bm")
-        t_bm = keep.tile([P, D], F32)
-        nc.scalar.activation(out=t_bm[:], in_=bm_ps.bitcast(BF16), func=ACT.Copy, scale=t32[:, 0:1])
         v_banks = product(nc, psum, xq_codes, xq_scales, wv_words, wv_planes, "v")
         m_banks = product(nc, psum, xq_codes, xq_scales, wm_words, wm_planes, "m")
 
@@ -163,22 +162,22 @@ def tile_diffscm_pb_s_kernel(
             )
         for cols in halves:
             nc.vector.scalar_tensor_tensor(
-                out=base[:, cols], in0=x_sb[:, cols], scalar=one_minus_t[:, 0:1],
-                in1=t_bm[:, cols], op0=ALU.mult, op1=ALU.add,
+                out=base[:, cols], in0=bm_ps.bitcast(BF16)[:, cols], scalar=t_bf[:, 0:1],
+                in1=x_part[:, cols], op0=ALU.mult, op1=ALU.add,
             )
         for cols in halves:
             nc.vector.scalar_tensor_tensor(
-                out=side[:, cols], in0=ramp[:, cols], scalar=t32[:, 0:1], in1=base[:, cols],
+                out=side[:, cols], in0=ramp[:, cols], scalar=t_bf[:, 0:1], in1=base[:, cols],
                 op0=ALU.mult, op1=ALU.add,
             )
         for h, cols in enumerate(halves):
             nc.vector.scalar_tensor_tensor(
-                out=rest[:, cols], in0=m_banks[h][:], scalar=t32[:, 0:1], in1=side[:, cols],
+                out=rest[:, cols], in0=m_banks[h][:], scalar=t_bf[:, 0:1], in1=side[:, cols],
                 op0=ALU.mult, op1=ALU.add,
             )
         for cols in halves:
             nc.vector.scalar_tensor_tensor(
-                out=tail[:, cols], in0=log_v[:, cols], scalar=t32[:, 0:1], in1=eps_sb[:, cols],
+                out=tail[:, cols], in0=log_v[:, cols], scalar=t_bf[:, 0:1], in1=eps_sb[:, cols],
                 op0=ALU.mult, op1=ALU.mult,
             )
         for cols in halves:

@@ -24,6 +24,8 @@ WORDS_PASS = K_PASS // 2
 SCALE_ROWS = 4
 BIAS_ROWS = D // (2 * P)
 
+WARM_UP = 4
+
 FLOPS = 2 * 2 * P * D * D
 
 
@@ -43,7 +45,8 @@ def load_weight(nc, keep, words_dram, scales_dram, label):
 def product(nc, psum, xq_codes, xq_scales, words, planes, label):
     banks = []
     for h in range(N_TILES):
-        bank = psum.tile([P, N_TILE], F32, name="%s_bank%d" % (label, h))
+        tag = "xt_bank0" if (label, h) == ("m", 1) else "%s_bank%d" % (label, h)
+        bank = psum.tile([P, N_TILE], F32, name="%s_bank%d" % (label, h), tag=tag)
         for g in range(PASSES):
             nc.tensor.matmul_mx(
                 out=bank[:],
@@ -67,10 +70,14 @@ def tile_diffscm_pb_s_kernel(
         psum = ctx.enter_context(tc.psum_pool(name="psum", bufs=1))
         ctx.enter_context(tc.manual_schedule())
 
+        zeros = keep.tile([P, P], F32)
+        nc.vector.memset(zeros[:], 0.0)
+        warm = psum.tile([P, P], F32, name="warm", tag="v_bank0")
+
         xt_sb = keep.tile([P, D], BF16)
         nc.sync.dma_start(out=xt_sb[:], in_=xt)
         bias_rows = keep.tile([P, 2 * P], BF16)
-        nc.vector.memset(bias_rows[:].bitcast(I32), 0)
+        nc.gpsimd.memset(bias_rows[:].bitcast(I32), 0)
         nc.sync.dma_start(out=bias_rows[0:BIAS_ROWS, :], in_=bv.rearrange("(r c) -> r c", r=BIAS_ROWS))
         nc.sync.dma_start(
             out=bias_rows[BIAS_ROWS : 2 * BIAS_ROWS, :], in_=bm.rearrange("(r c) -> r c", r=BIAS_ROWS)
@@ -95,31 +102,34 @@ def tile_diffscm_pb_s_kernel(
             out=x_part[:], in0=x_sb[:], scalar1=one_minus_t[:, 0:1], scalar2=0.0, op0=ALU.mult, op1=ALU.add
         )
 
+        for r in range(WARM_UP):
+            nc.tensor.matmul(warm[:], lhsT=zeros[:], rhs=zeros[:], start=True, stop=True)
         bias_cols_ps = psum.tile([P, P], F32)
         nc.tensor.transpose(bias_cols_ps[:], bias_rows[:].bitcast(F32), ident[:])
         xt_words = xt_sb[:].bitcast(F32)
-        xt_ps = psum.tile([P, PASSES, 2, P], F32)
+        xt_banks = []
         for g in range(PASSES):
+            bank = psum.tile([P, 2, P], F32, name="xt_bank%d" % g)
             for u in range(2):
                 nc.tensor.transpose(
-                    xt_ps[:, g, u, :],
+                    bank[:, u, :],
                     xt_words[:, WORDS_PASS * g + u : WORDS_PASS * (g + 1) : 2],
                     ident[:],
                 )
+            xt_banks.append(bank)
         bias_cols = keep.tile([P, 2 * BIAS_ROWS], F32)
         nc.scalar.copy(out=bias_cols[:], in_=bias_cols_ps[:, 0 : 2 * BIAS_ROWS])
 
         grouped = keep.tile([P, PASSES, P, PACK], BF16, align_bytes=64)
-        nc.vector.tensor_copy(
-            out=grouped[:].bitcast(F32), in_=xt_ps[:].rearrange("p g u b -> p g b u")
-        )
         xq_codes = keep.tile([P, PASSES, P], U32, align_bytes=64)
         xq_scales = keep.tile([P, PASSES, P], U8, align_bytes=64)
-        nc.vector.quantize_mx(
-            out=xq_codes[:].rearrange("p g b -> p (g b)").bitcast(FP8X4),
-            scales=xq_scales[:].rearrange("p g b -> p (g b)"),
-            in_=grouped[:].rearrange("p g b t -> p (g b t)"),
-        )
+        for g, copy in enumerate((nc.vector.tensor_copy, nc.scalar.copy)):
+            copy(out=grouped[:, g].bitcast(F32), in_=xt_banks[g][:].rearrange("p u b -> p b u"))
+            nc.vector.quantize_mx(
+                out=xq_codes[:, g, :].bitcast(FP8X4),
+                scales=xq_scales[:, g, :],
+                in_=grouped[:, g].rearrange("p b t -> p (b t)"),
+            )
 
         def spread_bias(first_row, label):
             bank = psum.tile([P, BIAS_ROWS, P], F32, name=label + "_ps")
@@ -131,8 +141,8 @@ def tile_diffscm_pb_s_kernel(
         bv_ps = spread_bias(0, "bv")
         bv_all = keep.tile([P, D], BF16)
         nc.scalar.copy(out=bv_all[:].bitcast(F32), in_=bv_ps)
-        bm_ps = spread_bias(BIAS_ROWS, "bm")
         v_banks = product(nc, psum, xq_codes, xq_scales, wv_words, wv_planes, "v")
+        bm_ps = spread_bias(BIAS_ROWS, "bm")
         m_banks = product(nc, psum, xq_codes, xq_scales, wm_words, wm_planes, "m")
 
         halves = [slice(N_TILE * h, N_TILE * (h + 1)) for h in range(N_TILES)]

@@ -167,13 +167,13 @@ def tile_diffscm_pb_s_kernel(
         result = keep.tile([P, D], F32)
         for cols in halves:
             nc.vector.scalar_tensor_tensor(
-                out=ramp[:, cols], in0=v[:, cols], scalar=0.0, in1=eps_sb[:, cols],
-                op0=ALU.max, op1=ALU.mult,
+                out=base[:, cols], in0=bm_ps.bitcast(BF16)[:, cols], scalar=t_bf[:, 0:1],
+                in1=x_part[:, cols], op0=ALU.mult, op1=ALU.add,
             )
         for cols in halves:
             nc.vector.scalar_tensor_tensor(
-                out=base[:, cols], in0=bm_ps.bitcast(BF16)[:, cols], scalar=t_bf[:, 0:1],
-                in1=x_part[:, cols], op0=ALU.mult, op1=ALU.add,
+                out=ramp[:, cols], in0=v[:, cols], scalar=0.0, in1=eps_sb[:, cols],
+                op0=ALU.max, op1=ALU.mult,
             )
         for cols in halves:
             nc.vector.scalar_tensor_tensor(

@@ -20,11 +20,10 @@ K_PASS = P * PACK
 PASSES = D // K_PASS
 N_TILE = 512
 N_TILES = D // N_TILE
+QUARTER = D // 4
 WORDS_PASS = K_PASS // 2
 SCALE_ROWS = 4
 BIAS_ROWS = D // (2 * P)
-
-WARM_UP = 4
 
 FLOPS = 2 * 2 * P * D * D
 
@@ -42,23 +41,21 @@ def load_weight(nc, keep, words_dram, scales_dram, label):
     return words, planes
 
 
-def product(nc, psum, xq_codes, xq_scales, words, planes, label):
-    banks = []
-    for h in range(N_TILES):
-        tag = "xt_bank0" if (label, h) == ("m", 1) else "%s_bank%d" % (label, h)
-        bank = psum.tile([P, N_TILE], F32, name="%s_bank%d" % (label, h), tag=tag)
-        for g in range(PASSES):
-            nc.tensor.matmul_mx(
-                out=bank[:],
-                lhsT=xq_codes[:, g, :].bitcast(FP8X4),
-                lhsT_scale=xq_scales[:, g, :],
-                rhs=words[:, g, 2 * N_TILE * h : 2 * N_TILE * (h + 1)].bitcast(FP4X4),
-                rhs_scale=planes[:, g, N_TILE * h : N_TILE * (h + 1)],
-                start=(g == 0),
-                stop=(g == PASSES - 1),
-            )
-        banks.append(bank)
-    return banks
+def product(nc, banks, n_pass, xq_codes, xq_scales, words, planes):
+    width = D // len(banks)
+    for i, bank in enumerate(banks):
+        for c in range(0, width, n_pass):
+            n = width * i + c
+            for g in range(PASSES):
+                nc.tensor.matmul_mx(
+                    out=bank[:, c : c + n_pass],
+                    lhsT=xq_codes[:, g, :].bitcast(FP8X4),
+                    lhsT_scale=xq_scales[:, g, :],
+                    rhs=words[:, g, 2 * n : 2 * (n + n_pass)].bitcast(FP4X4),
+                    rhs_scale=planes[:, g, n : n + n_pass],
+                    start=(g == 0),
+                    stop=(g == PASSES - 1),
+                )
 
 
 def tile_diffscm_pb_s_kernel(
@@ -69,10 +66,6 @@ def tile_diffscm_pb_s_kernel(
         keep = ctx.enter_context(tc.tile_pool(name="keep", bufs=1))
         psum = ctx.enter_context(tc.psum_pool(name="psum", bufs=1))
         ctx.enter_context(tc.manual_schedule())
-
-        zeros = keep.tile([P, P], F32)
-        nc.vector.memset(zeros[:], 0.0)
-        warm = psum.tile([P, P], F32, name="warm", tag="v_bank0")
 
         xt_sb = keep.tile([P, D], BF16)
         nc.sync.dma_start(out=xt_sb[:], in_=xt)
@@ -98,18 +91,18 @@ def tile_diffscm_pb_s_kernel(
             out=one_minus_t[:], in0=t_bf[:], scalar1=-1.0, scalar2=1.0, op0=ALU.mult, op1=ALU.add
         )
         x_part = keep.tile([P, D], F32)
-        nc.gpsimd.tensor_scalar(
-            out=x_part[:], in0=x_sb[:], scalar1=one_minus_t[:, 0:1], scalar2=0.0, op0=ALU.mult, op1=ALU.add
-        )
+        for cols in (slice(0, QUARTER), slice(QUARTER, D)):
+            nc.gpsimd.tensor_scalar(
+                out=x_part[:, cols], in0=x_sb[:, cols], scalar1=one_minus_t[:, 0:1], scalar2=0.0,
+                op0=ALU.mult, op1=ALU.add,
+            )
 
-        for r in range(WARM_UP):
-            nc.tensor.matmul(warm[:], lhsT=zeros[:], rhs=zeros[:], start=True, stop=True)
-        bias_cols_ps = psum.tile([P, P], F32)
-        nc.tensor.transpose(bias_cols_ps[:], bias_rows[:].bitcast(F32), ident[:])
+        bias_cols_ps = psum.tile([P, N_TILE], F32)
+        nc.tensor.transpose(bias_cols_ps[:, 0:P], bias_rows[:].bitcast(F32), ident[:])
         xt_words = xt_sb[:].bitcast(F32)
         xt_banks = []
         for g in range(PASSES):
-            bank = psum.tile([P, 2, P], F32, name="xt_bank%d" % g)
+            bank = psum.tile([P, PACK, P], F32, name="xt_bank%d" % g)
             for u in range(2):
                 nc.tensor.transpose(
                     bank[:, u, :],
@@ -124,52 +117,73 @@ def tile_diffscm_pb_s_kernel(
         xq_codes = keep.tile([P, PASSES, P], U32, align_bytes=64)
         xq_scales = keep.tile([P, PASSES, P], U8, align_bytes=64)
         for g, copy in enumerate((nc.vector.tensor_copy, nc.scalar.copy)):
-            copy(out=grouped[:, g].bitcast(F32), in_=xt_banks[g][:].rearrange("p u b -> p b u"))
+            copy(out=grouped[:, g].bitcast(F32), in_=xt_banks[g][:, 0:2].rearrange("p u b -> p b u"))
             nc.vector.quantize_mx(
                 out=xq_codes[:, g, :].bitcast(FP8X4),
                 scales=xq_scales[:, g, :],
                 in_=grouped[:, g].rearrange("p b t -> p (b t)"),
             )
 
-        def spread_bias(first_row, label):
-            bank = psum.tile([P, BIAS_ROWS, P], F32, name=label + "_ps")
-            for r in range(BIAS_ROWS):
-                column = bias_cols[:, first_row + r : first_row + r + 1]
-                nc.tensor.transpose(bank[:, r, :], column.to_broadcast([P, P]), ident[:])
-            return bank[:].rearrange("p r j -> p (r j)")
+        def spread_row(words, row):
+            column = bias_cols[:, row : row + 1]
+            nc.tensor.transpose(words, column.to_broadcast([P, P]), ident[:])
 
-        bv_ps = spread_bias(0, "bv")
+        bv_ps = psum.tile([P, BIAS_ROWS, P], F32)
+        for r in range(BIAS_ROWS):
+            spread_row(bv_ps[:, r, :], r)
         bv_all = keep.tile([P, D], BF16)
-        nc.scalar.copy(out=bv_all[:].bitcast(F32), in_=bv_ps)
-        v_banks = product(nc, psum, xq_codes, xq_scales, wv_words, wv_planes, "v")
-        bm_ps = spread_bias(BIAS_ROWS, "bm")
-        m_banks = product(nc, psum, xq_codes, xq_scales, wm_words, wm_planes, "m")
+        nc.scalar.copy(out=bv_all[:].bitcast(F32), in_=bv_ps[:].rearrange("p r j -> p (r j)"))
+        v_tags = ("v_bank0", "v_bank1", "bias_cols_ps", "v_bank3")
+        v_banks = [psum.tile([P, N_TILE], F32, name="v_quarter%d" % i, tag=tag) for i, tag in enumerate(v_tags)]
+        bm_first = v_banks[0][:, N_TILE - P :]
+        spread_row(bm_first, BIAS_ROWS)
+        product(nc, v_banks, P, xq_codes, xq_scales, wv_words, wv_planes)
+        bm_ps = psum.tile([P, BIAS_ROWS, P], F32)
+        for r in range(1, BIAS_ROWS):
+            spread_row(bm_ps[:, r, :], BIAS_ROWS + r)
+        bm_all = bm_ps[:].rearrange("p r j -> p (r j)").bitcast(BF16)
+        m_banks = [psum.tile([P, N_TILE], F32, name="m_half%d" % i, tag="xt_bank%d" % i) for i in range(N_TILES)]
+        product(nc, m_banks, N_TILE, xq_codes, xq_scales, wm_words, wm_planes)
 
         halves = [slice(N_TILE * h, N_TILE * (h + 1)) for h in range(N_TILES)]
         v = keep.tile([P, D], F32)
         abs_v = keep.tile([P, D], F32)
         exp_v = keep.tile([P, D], F32)
         log_v = keep.tile([P, D], F32)
-        for h, cols in enumerate(halves):
-            nc.vector.tensor_tensor(out=v[:, cols], in0=v_banks[h][:], in1=bv_all[:, cols], op=ALU.add)
-        for cols in halves:
+        quarters = [slice(QUARTER * i, QUARTER * (i + 1)) for i in range(D // QUARTER)]
+        base = keep.tile([P, D], F32)
+
+        def add_base(cols, bm_part):
+            nc.vector.scalar_tensor_tensor(
+                out=base[:, cols], in0=bm_part, scalar=t_bf[:, 0:1],
+                in1=x_part[:, cols], op0=ALU.mult, op1=ALU.add,
+            )
+
+        for i, cols in enumerate(quarters):
+            if i == 3:
+                add_base(quarters[0], bm_first.bitcast(BF16))
+            nc.vector.tensor_tensor(
+                out=v[:, cols], in0=v_banks[i][:, 0:QUARTER], in1=bv_all[:, cols], op=ALU.add
+            )
+        for i, cols in enumerate(quarters):
             nc.scalar.activation(out=abs_v[:, cols], in_=v[:, cols], func=ACT.Abs)
-        for cols in halves:
-            nc.scalar.activation(out=exp_v[:, cols], in_=abs_v[:, cols], func=ACT.Exp, scale=-1.0)
+            if i > 0:
+                nc.scalar.activation(
+                    out=exp_v[:, quarters[i - 1]], in_=abs_v[:, quarters[i - 1]], func=ACT.Exp, scale=-1.0
+                )
+        nc.scalar.activation(
+            out=exp_v[:, quarters[-1]], in_=abs_v[:, quarters[-1]], func=ACT.Exp, scale=-1.0
+        )
         for cols in halves:
             nc.scalar.activation(out=log_v[:, cols], in_=exp_v[:, cols], func=ACT.Ln, bias=1.0)
 
         ramp = keep.tile([P, D], F32)
-        base = keep.tile([P, D], F32)
         side = keep.tile([P, D], F32)
         rest = keep.tile([P, D], F32)
         tail = keep.tile([P, D], F32)
         result = keep.tile([P, D], F32)
-        for cols in halves:
-            nc.vector.scalar_tensor_tensor(
-                out=base[:, cols], in0=bm_ps.bitcast(BF16)[:, cols], scalar=t_bf[:, 0:1],
-                in1=x_part[:, cols], op0=ALU.mult, op1=ALU.add,
-            )
+        for cols in (quarters[1], halves[1]):
+            add_base(cols, bm_all[:, cols])
         for cols in halves:
             nc.vector.scalar_tensor_tensor(
                 out=ramp[:, cols], in0=v[:, cols], scalar=0.0, in1=eps_sb[:, cols],

from contextlib import ExitStack

import concourse.mybir as mybir
from concourse.masks import make_identity

F32 = mybir.dt.float32
BF16 = mybir.dt.bfloat16
I32 = mybir.dt.int32
U32 = mybir.dt.uint32
U8 = mybir.dt.uint8
FP8X4 = mybir.dt.float8_e4m3fn_x4
FP4X4 = mybir.dt.float4_e2m1fn_x4
ALU = mybir.AluOpType
ACT = mybir.ActivationFunctionType

P = 128
D = 1024
PACK = 4
K_PASS = P * PACK
PASSES = D // K_PASS
N_TILE = 512
N_TILES = D // N_TILE
QUARTER = D // 4
WORDS_PASS = K_PASS // 2
SCALE_ROWS = 4
BIAS_ROWS = D // (2 * P)

FLOPS = 2 * 2 * P * D * D


def load_weight(nc, keep, words_dram, scales_dram, label):
    planes = keep.tile([P, PASSES, D], U8, name=label + "_planes", align_bytes=64)
    words = keep.tile([P, PASSES, 2 * D], U8, name=label + "_words", align_bytes=64)
    nc.vector.memset(planes[:].bitcast(I32), 0)
    rows = scales_dram.bitcast(I32).rearrange("g (q r) n -> r q g n", r=SCALE_ROWS)
    for r in range(SCALE_ROWS):
        nc.sync.dma_start(out=planes[r:P:32].bitcast(I32), in_=rows[r])
    nc.sync.dma_start(
        out=words[:].bitcast(I32), in_=words_dram.bitcast(I32).rearrange("g p w -> p g w")
    )
    return words, planes


def product(nc, banks, n_pass, xq_codes, xq_scales, words, planes):
    width = D // len(banks)
    for i, bank in enumerate(banks):
        for c in range(0, width, n_pass):
            n = width * i + c
            for g in range(PASSES):
                nc.tensor.matmul_mx(
                    out=bank[:, c : c + n_pass],
                    lhsT=xq_codes[:, g, :].bitcast(FP8X4),
                    lhsT_scale=xq_scales[:, g, :],
                    rhs=words[:, g, 2 * n : 2 * (n + n_pass)].bitcast(FP4X4),
                    rhs_scale=planes[:, g, n : n + n_pass],
                    start=(g == 0),
                    stop=(g == PASSES - 1),
                )


def tile_diffscm_pb_s_kernel(
    tc, xt, eps, x, t_rand, Wm_words, Wm_scales, bm, Wv_words, Wv_scales, bv, out
):
    nc = tc.nc
    with ExitStack() as ctx:
        keep = ctx.enter_context(tc.tile_pool(name="keep", bufs=1))
        psum = ctx.enter_context(tc.psum_pool(name="psum", bufs=1))
        ctx.enter_context(tc.manual_schedule())

        xt_sb = keep.tile([P, D], BF16)
        nc.sync.dma_start(out=xt_sb[:], in_=xt)
        bias_rows = keep.tile([P, 2 * P], BF16)
        nc.gpsimd.memset(bias_rows[:].bitcast(I32), 0)
        nc.sync.dma_start(out=bias_rows[0:BIAS_ROWS, :], in_=bv.rearrange("(r c) -> r c", r=BIAS_ROWS))
        nc.sync.dma_start(
            out=bias_rows[BIAS_ROWS : 2 * BIAS_ROWS, :], in_=bm.rearrange("(r c) -> r c", r=BIAS_ROWS)
        )
        wv_words, wv_planes = load_weight(nc, keep, Wv_words, Wv_scales, "wv")
        t_bf = keep.tile([P, 1], BF16)
        nc.sync.dma_start(out=t_bf[:], in_=t_rand)
        wm_words, wm_planes = load_weight(nc, keep, Wm_words, Wm_scales, "wm")

        ident = keep.tile([P, P], F32)
        make_identity(nc, ident[:])
        x_sb = keep.tile([P, D], BF16)
        nc.gpsimd.dma_start(out=x_sb[:], in_=x)
        eps_sb = keep.tile([P, D], BF16)
        nc.gpsimd.dma_start(out=eps_sb[:], in_=eps)
        one_minus_t = keep.tile([P, 1], F32)
        nc.gpsimd.tensor_scalar(
            out=one_minus_t[:], in0=t_bf[:], scalar1=-1.0, scalar2=1.0, op0=ALU.mult, op1=ALU.add
        )
        x_part = keep.tile([P, D], F32)
        for cols in (slice(0, QUARTER), slice(QUARTER, D)):
            nc.gpsimd.tensor_scalar(
                out=x_part[:, cols], in0=x_sb[:, cols], scalar1=one_minus_t[:, 0:1], scalar2=0.0,
                op0=ALU.mult, op1=ALU.add,
            )

        bias_cols_ps = psum.tile([P, N_TILE], F32)
        nc.tensor.transpose(bias_cols_ps[:, 0:P], bias_rows[:].bitcast(F32), ident[:])
        xt_words = xt_sb[:].bitcast(F32)
        xt_banks = []
        for g in range(PASSES):
            bank = psum.tile([P, PACK, P], F32, name="xt_bank%d" % g)
            for u in range(2):
                nc.tensor.transpose(
                    bank[:, u, :],
                    xt_words[:, WORDS_PASS * g + u : WORDS_PASS * (g + 1) : 2],
                    ident[:],
                )
            xt_banks.append(bank)
        bias_cols = keep.tile([P, 2 * BIAS_ROWS], F32)
        nc.scalar.copy(out=bias_cols[:], in_=bias_cols_ps[:, 0 : 2 * BIAS_ROWS])

        grouped = keep.tile([P, PASSES, P, PACK], BF16, align_bytes=64)
        xq_codes = keep.tile([P, PASSES, P], U32, align_bytes=64)
        xq_scales = keep.tile([P, PASSES, P], U8, align_bytes=64)
        for g, copy in enumerate((nc.vector.tensor_copy, nc.scalar.copy)):
            copy(out=grouped[:, g].bitcast(F32), in_=xt_banks[g][:, 0:2].rearrange("p u b -> p b u"))
            nc.vector.quantize_mx(
                out=xq_codes[:, g, :].bitcast(FP8X4),
                scales=xq_scales[:, g, :],
                in_=grouped[:, g].rearrange("p b t -> p (b t)"),
            )

        def spread_row(words, row):
            column = bias_cols[:, row : row + 1]
            nc.tensor.transpose(words, column.to_broadcast([P, P]), ident[:])

        bv_ps = psum.tile([P, BIAS_ROWS, P], F32)
        for r in range(BIAS_ROWS):
            spread_row(bv_ps[:, r, :], r)
        bv_all = keep.tile([P, D], BF16)
        nc.scalar.copy(out=bv_all[:].bitcast(F32), in_=bv_ps[:].rearrange("p r j -> p (r j)"))
        v_tags = ("v_bank0", "v_bank1", "bias_cols_ps", "v_bank3")
        v_banks = [psum.tile([P, N_TILE], F32, name="v_quarter%d" % i, tag=tag) for i, tag in enumerate(v_tags)]
        bm_first = v_banks[0][:, N_TILE - P :]
        spread_row(bm_first, BIAS_ROWS)
        product(nc, v_banks, P, xq_codes, xq_scales, wv_words, wv_planes)
        bm_ps = psum.tile([P, BIAS_ROWS, P], F32)
        for r in range(1, BIAS_ROWS):
            spread_row(bm_ps[:, r, :], BIAS_ROWS + r)
        bm_all = bm_ps[:].rearrange("p r j -> p (r j)").bitcast(BF16)
        m_banks = [psum.tile([P, N_TILE], F32, name="m_half%d" % i, tag="xt_bank%d" % i) for i in range(N_TILES)]
        product(nc, m_banks, N_TILE, xq_codes, xq_scales, wm_words, wm_planes)

        halves = [slice(N_TILE * h, N_TILE * (h + 1)) for h in range(N_TILES)]
        v = keep.tile([P, D], F32)
        abs_v = keep.tile([P, D], F32)
        exp_v = keep.tile([P, D], F32)
        log_v = keep.tile([P, D], F32)
        quarters = [slice(QUARTER * i, QUARTER * (i + 1)) for i in range(D // QUARTER)]
        base = keep.tile([P, D], F32)

        def add_base(cols, bm_part):
            nc.vector.scalar_tensor_tensor(
                out=base[:, cols], in0=bm_part, scalar=t_bf[:, 0:1],
                in1=x_part[:, cols], op0=ALU.mult, op1=ALU.add,
            )

        for i, cols in enumerate(quarters):
            if i == 3:
                add_base(quarters[0], bm_first.bitcast(BF16))
            nc.vector.tensor_tensor(
                out=v[:, cols], in0=v_banks[i][:, 0:QUARTER], in1=bv_all[:, cols], op=ALU.add
            )
        for i, cols in enumerate(quarters):
            nc.scalar.activation(out=abs_v[:, cols], in_=v[:, cols], func=ACT.Abs)
            if i > 0:
                nc.scalar.activation(
                    out=exp_v[:, quarters[i - 1]], in_=abs_v[:, quarters[i - 1]], func=ACT.Exp, scale=-1.0
                )
        nc.scalar.activation(
            out=exp_v[:, quarters[-1]], in_=abs_v[:, quarters[-1]], func=ACT.Exp, scale=-1.0
        )
        for cols in halves:
            nc.scalar.activation(out=log_v[:, cols], in_=exp_v[:, cols], func=ACT.Ln, bias=1.0)

        ramp = keep.tile([P, D], F32)
        side = keep.tile([P, D], F32)
        rest = keep.tile([P, D], F32)
        tail = keep.tile([P, D], F32)
        result = keep.tile([P, D], F32)
        for cols in (quarters[1], halves[1]):
            add_base(cols, bm_all[:, cols])
        for cols in halves:
            nc.vector.scalar_tensor_tensor(
                out=ramp[:, cols], in0=v[:, cols], scalar=0.0, in1=eps_sb[:, cols],
                op0=ALU.max, op1=ALU.mult,
            )
        for cols in halves:
            nc.vector.scalar_tensor_tensor(
                out=side[:, cols], in0=ramp[:, cols], scalar=t_bf[:, 0:1], in1=base[:, cols],
                op0=ALU.mult, op1=ALU.add,
            )
        for h, cols in enumerate(halves):
            nc.vector.scalar_tensor_tensor(
                out=rest[:, cols], in0=m_banks[h][:], scalar=t_bf[:, 0:1], in1=side[:, cols],
                op0=ALU.mult, op1=ALU.add,
            )
        for cols in halves:
            nc.vector.scalar_tensor_tensor(
                out=tail[:, cols], in0=log_v[:, cols], scalar=t_bf[:, 0:1], in1=eps_sb[:, cols],
                op0=ALU.mult, op1=ALU.mult,
            )
        for cols in halves:
            nc.vector.tensor_tensor(out=result[:, cols], in0=tail[:, cols], in1=rest[:, cols], op=ALU.add)
            nc.sync.dma_start(out=out[:, cols], in_=result[:, cols])
